import numpy as np
import ml_dtypes


def mxq(x, axis, fmt="e4m3"):
    dtype, down = {"e4m3": (ml_dtypes.float8_e4m3fn, 7), "e5m2": (ml_dtypes.float8_e5m2, 14)}[fmt]
    v = np.moveaxis(np.asarray(x, np.float32).astype(ml_dtypes.bfloat16).astype(np.float64), axis, -1)
    blocks = v.reshape(v.shape[:-1] + (-1, 32))
    amax = np.abs(blocks).max(-1, keepdims=True)
    byte = np.maximum(np.where(amax > 0, np.frexp(amax)[1] - 1 + 127, 0) - down, 1)
    scale = np.exp2(byte - 127.0)
    codes = (blocks / scale).astype(np.float32).astype(dtype).astype(np.float64)
    return np.moveaxis((codes * scale).reshape(v.shape), -1, axis)


WIDE = False


def mx_kscale(k):
    if not WIDE:
        return np.ones(k)
    levels = np.array([10, -10, 5, -5, 0])
    a = np.random.permutation(np.resize(levels, k // 512 * 4)).reshape(k // 512, 4)
    idx = np.arange(k)
    return np.exp2(a[idx // 512, idx % 128 // 32])


BF16 = ml_dtypes.bfloat16


def bf(x):
    return np.asarray(x, np.float32).astype(BF16)


def f64(x):
    return np.asarray(x).astype(np.float64)


E2M1 = np.array([0.0, 0.5, 1.0, 1.5, 2.0, 3.0, 4.0, 6.0, -0.0, -0.5, -1.0, -1.5, -2.0, -3.0, -4.0, -6.0])


def pack_weight(w, fmt):
    k, n = w.shape
    w = f64(bf(w)).reshape(k // 32, 32, n)
    amax = np.abs(w).max(1)
    if fmt == "e4m3":
        byte = np.frexp(amax)[1] - 1 + 127 - 7
    else:
        mant, ex = np.frexp(amax / 6.0)
        byte = np.where(mant > 0.5, ex, ex - 1) + 127
    byte = np.clip(np.where(amax > 0, byte, 1), 1, 254)
    scaled = (w * np.exp2(127.0 - byte)[:, None, :]).reshape(k, n).astype(np.float32)
    by_word = np.ascontiguousarray(scaled.reshape(k // 512, 128, 4, n).transpose(0, 1, 3, 2))
    if fmt == "e4m3":
        words = by_word.astype(ml_dtypes.float8_e4m3fn).view(np.uint8)
    else:
        c = by_word.astype(ml_dtypes.float4_e2m1fn).view(np.uint8) & 0xF
        words = c[..., 0::2] | (c[..., 1::2] << 4)
    return np.ascontiguousarray(words), np.ascontiguousarray(byte.astype(np.uint8).reshape(k // 512, 16, n))


def unpack_weight(words, scales, fmt):
    g, p, n, _ = words.shape
    if fmt == "e4m3":
        vals = np.ascontiguousarray(words).view(ml_dtypes.float8_e4m3fn).astype(np.float64)
    else:
        nib = np.empty((g, p, n, 4), np.uint8)
        nib[..., 0::2] = words & 0xF
        nib[..., 1::2] = words >> 4
        vals = E2M1[nib]
    vals = vals * np.repeat(np.exp2(scales.astype(np.float64) - 127.0), 8, axis=1)[..., None]
    return vals.transpose(0, 1, 3, 2).reshape(g * 512, n)


B, N, D, L = 4, 1024, 512, 3
GAIN = 8.0


def setup_inputs():
    s, t = mx_kscale(N), mx_kscale(D)
    c = np.exp2(np.round(np.log2(np.mean(1.0 / s))))
    sc = s * c
    deg = np.exp2(np.random.uniform(-1.0, 2.0, (B, N, 1)))
    adj = deg * np.exp(2.0 * np.random.standard_normal((B, N, N)) - 2.0) / N
    x = bf(np.random.standard_normal((B, N, D)) * sc[:, None] * t)
    adj = bf(adj / sc)
    w_words, w_scales = pack_weight(np.random.standard_normal((D, D)) * GAIN / np.sqrt(D) / t[:, None], "e4m3")
    b = bf(np.random.standard_normal(D) * 0.5)
    return {"x": x,
            "adj": adj,
            "w_words": w_words,
            "w_scales": w_scales,
            "b": b}


def reference(x, adj, w_words, w_scales, b):
    a = f64(adj)
    denom = a.sum(axis=2, keepdims=True) + 1.0
    ax = mxq(a, 2, "e4m3") @ mxq(f64(x), 1, "e4m3")
    axw = (mxq(ax, 2, "e4m3") @ unpack_weight(w_words, w_scales, "e4m3")) + f64(b)
    return np.maximum(axw / denom, 0.0)

@@ -1,0 +1,311 @@
+from contextlib import ExitStack
+
+import concourse.mybir as mybir
+from concourse.masks import make_identity
+
+BF16 = mybir.dt.bfloat16
+F32 = mybir.dt.float32
+I32 = mybir.dt.int32
+U32 = mybir.dt.uint32
+U8 = mybir.dt.uint8
+FP8X4 = mybir.dt.float8_e4m3fn_x4
+ALU = mybir.AluOpType
+RELU = mybir.ActivationFunctionType.Relu
+
+P = 128
+PACK = 4
+K_PASS = P * PACK
+GRAPHS = 4
+NODES = 1024
+FEATS = 512
+J_PASSES = NODES // K_PASS
+TILES = NODES // P
+UNIT_TILES = 2
+UNIT_NODES = UNIT_TILES * P
+UNITS_PER_GRAPH = TILES // UNIT_TILES
+ALL_UNITS = GRAPHS * UNITS_PER_GRAPH
+QUARTER = P // PACK
+QUARTERS = P // QUARTER
+
+LAG_QUANTISE_ADJ = 1
+LAG_AGGREGATE = 2
+LAG_QUANTISE_AX = 3
+LAG_TRANSFORM = 4
+LAG_RECIPROCAL = UNITS_PER_GRAPH + 1
+LAG_FINISH = LAG_RECIPROCAL + 1
+X_LEAD = 1
+
+FLOPS = 2 * GRAPHS * NODES * NODES * FEATS + 2 * GRAPHS * NODES * FEATS * FEATS
+
+
+def tile_msamodel_pa_kernel(tc, x, adj, w_words, w_scales, b, out):
+    nc = tc.nc
+    with ExitStack() as ctx:
+        ctx.enter_context(tc.manual_schedule())
+        consts = ctx.enter_context(tc.tile_pool(name="consts", bufs=1))
+        inputs = ctx.enter_context(tc.tile_pool(name="inputs", bufs=1))
+        stream = ctx.enter_context(tc.tile_pool(name="stream", bufs=3))
+        psum = ctx.enter_context(tc.psum_pool(name="psum", bufs=2))
+
+        def graph_of(unit):
+            return unit // UNITS_PER_GRAPH
+
+        def first_tile_of(unit):
+            return (unit % UNITS_PER_GRAPH) * UNIT_TILES
+
+        w_plane = consts.tile([P, FEATS], U8, align_bytes=64)
+        nc.vector.memset(w_plane[:].bitcast(I32), 0)
+        w_codes = consts.tile([P, FEATS * PACK], U8, align_bytes=64)
+        selectors = consts.tile([P, QUARTERS, P], F32)
+        nc.vector.memset(selectors[:], 0.0)
+        bias_row = consts.tile([P, FEATS], BF16)
+        nc.gpsimd.memset(bias_row[:], 0.0)
+        ones = consts.tile([P, P], BF16)
+        nc.gpsimd.memset(ones[:], 1.0)
+        identity = consts.tile([P, P], F32)
+        make_identity(nc, identity[:])
+
+        x_rows = {}
+        adj_rows = {}
+
+        def load_x(g):
+            for c in range(J_PASSES):
+                rows = inputs.tile([P, PACK, FEATS], BF16, name="x_rows_%d_%d" % (g, c))
+                x_rows[(g, c)] = rows
+                nc.sync.dma_start(
+                    out=rows[:].rearrange("q (u e) d -> q u (e d)", e=2),
+                    in_=x[g, c * K_PASS : (c + 1) * K_PASS, :].rearrange("(u q e) d -> q u (e d)", q=P, e=2),
+                )
+
+        def load_adj(unit):
+            first = first_tile_of(unit)
+            rows = inputs.tile([P, UNIT_TILES, NODES], BF16, name="adj_rows_%d" % unit)
+            adj_rows[unit] = rows
+            by_tile = adj[graph_of(unit)].rearrange("(m a) j -> m a j", a=TILES)
+            nc.sync.dma_start(out=rows[:], in_=by_tile[:, first : first + UNIT_TILES, :])
+
+        def load_weight():
+            for quadrant in range(PACK):
+                nc.sync.dma_start(
+                    out=w_plane[32 * quadrant : 32 * quadrant + PACK, :].bitcast(I32),
+                    in_=w_scales[0, PACK * quadrant : PACK * (quadrant + 1), :].bitcast(I32),
+                )
+            nc.sync.dma_start(
+                out=w_codes[:].bitcast(I32),
+                in_=w_words[0].rearrange("p n t -> p (n t)").bitcast(I32),
+            )
+
+        load_x(0)
+        nc.sync.dma_start(out=bias_row[0:1, :], in_=b.unsqueeze(0))
+        for unit in range(UNITS_PER_GRAPH):
+            load_adj(unit)
+        load_x(1)
+        load_weight()
+        for g in range(1, GRAPHS):
+            for unit in range(g * UNITS_PER_GRAPH, (g + 1) * UNITS_PER_GRAPH):
+                load_adj(unit)
+            if g + 1 < GRAPHS:
+                load_x(g + 1)
+
+        for s in range(QUARTERS):
+            nc.vector.tensor_reduce(
+                out=selectors[:, s, s * QUARTER : (s + 1) * QUARTER],
+                in_=identity[:].rearrange("k (r t) -> k r t", t=PACK),
+                axis=mybir.AxisListType.X,
+                op=ALU.add,
+            )
+
+        bias_bank = psum.tile([P, FEATS], F32, name="bias_bank", tag="out_bank")
+        nc.tensor.matmul(out=bias_bank[:], lhsT=ones[:], rhs=bias_row[:], start=True, stop=True)
+        bias_all = consts.tile([P, FEATS], F32)
+        nc.scalar.copy(out=bias_all[:], in_=bias_bank[:])
+
+        x_grouped = {}
+        x_codes = {}
+        x_scales = {}
+        adj_grouped = {}
+        adj_codes = {}
+        adj_scales = {}
+        row_sums = {}
+        partial_sums = {}
+        reciprocals = {}
+        ax_grouped = {}
+        ax_codes = {}
+        ax_scales = {}
+        results = {}
+
+        def regroup_x(g, c):
+            if c == 0:
+                x_grouped[g] = stream.tile(
+                    [P, J_PASSES, PACK, P, PACK], BF16, name="x_grouped", tag="x_grouped", bufs=2, align_bytes=64
+                )
+            nc.vector.tensor_copy(
+                out=x_grouped[g][:, c],
+                in_=x_rows[(g, c)][:].rearrange("q t (p r) -> q r p t", r=PACK),
+            )
+
+        def quantise_x(g):
+            x_codes[g] = stream.tile([P, J_PASSES, FEATS], U32, name="x_codes", tag="x_codes", bufs=2, align_bytes=64)
+            x_scales[g] = stream.tile([P, J_PASSES, FEATS], U8, name="x_scales", tag="x_scales", bufs=2, align_bytes=64)
+            nc.vector.quantize_mx(
+                out=x_codes[g][:].rearrange("q c f -> q (c f)").bitcast(FP8X4),
+                scales=x_scales[g][:].rearrange("q c f -> q (c f)"),
+                in_=x_grouped[g][:].rearrange("q c r p t -> q (c r p t)"),
+            )
+
+        def prepare_x(turn):
+            g = turn // UNITS_PER_GRAPH
+            part = turn % UNITS_PER_GRAPH
+            if part < J_PASSES:
+                regroup_x(g, part)
+            elif part == J_PASSES:
+                quantise_x(g)
+
+        def transpose_adj(unit):
+            words = adj_rows[unit][:].bitcast(F32)
+            grouped = stream.tile(
+                [P, J_PASSES, UNIT_NODES, PACK], BF16, name="adj_grouped", tag="adj_grouped", align_bytes=64
+            )
+            adj_grouped[unit] = grouped
+            for c in range(J_PASSES):
+                flipped = psum.tile([P, 2, UNIT_NODES], F32, name="flipped", tag="flipped")
+                for u in range(2):
+                    block = 2 * c + u
+                    for k in range(UNIT_TILES):
+                        nc.tensor.transpose(
+                            flipped[:, u, k * P : (k + 1) * P],
+                            words[:, k, block * P : (block + 1) * P],
+                            identity[:],
+                        )
+                nc.scalar.copy(out=grouped[:, c].bitcast(F32), in_=flipped[:].rearrange("q u w -> q w u"))
+
+        def quantise_adj(unit):
+            adj_codes[unit] = stream.tile(
+                [P, J_PASSES, UNIT_NODES], U32, name="adj_codes", tag="adj_codes", bufs=4, align_bytes=64
+            )
+            adj_scales[unit] = stream.tile(
+                [P, J_PASSES, UNIT_NODES], U8, name="adj_scales", tag="adj_scales", bufs=4, align_bytes=64
+            )
+            nc.vector.quantize_mx(
+                out=adj_codes[unit][:].rearrange("q c w -> q (c w)").bitcast(FP8X4),
+                scales=adj_scales[unit][:].rearrange("q c w -> q (c w)"),
+                in_=adj_grouped[unit][:].rearrange("q c w t -> q (c w t)"),
+            )
+
+        def add_row_sums(unit):
+            g = graph_of(unit)
+            if unit % UNITS_PER_GRAPH == 0:
+                row_sums[g] = psum.tile([P, QUARTERS, TILES], F32, name="row_sums", tag="row_sums", bufs=1)
+            for k in range(UNIT_TILES):
+                a = first_tile_of(unit) + k
+                for s in range(QUARTERS):
+                    first = k * P + s * QUARTER
+                    for c in range(J_PASSES):
+                        nc.tensor.matmul(
+                            out=row_sums[g][:, s, a : a + 1],
+                            lhsT=adj_grouped[unit][:, c, first : first + QUARTER, :].rearrange("q w t -> q (w t)"),
+                            rhs=ones[:, 0:1],
+                            start=(c == 0),
+                            stop=(c == J_PASSES - 1),
+                        )
+
+        def collect_row_sums(g):
+            partial_sums[g] = stream.tile([P, QUARTERS, TILES], F32, name="partial_sums", tag="partial_sums")
+            nc.vector.tensor_copy(out=partial_sums[g][:], in_=row_sums[g][:])
+
+        def reciprocal_denominators(g):
+            totals = psum.tile([P, TILES], F32, name="totals", tag="totals", bufs=1)
+            for s in range(QUARTERS):
+                nc.tensor.matmul(
+                    out=totals[:],
+                    lhsT=selectors[:, s, :],
+                    rhs=partial_sums[g][:, s, :],
+                    start=(s == 0),
+                    stop=(s == QUARTERS - 1),
+                )
+            denominators = stream.tile([P, TILES], F32, name="denominators", tag="denominators")
+            nc.vector.tensor_scalar_add(out=denominators[:], in0=totals[:], scalar1=1.0)
+            reciprocals[g] = stream.tile([P, TILES], F32, name="reciprocals", tag="reciprocals")
+            nc.vector.reciprocal(out=reciprocals[g][:], in_=denominators[:])
+
+        def aggregate(unit):
+            g = graph_of(unit)
+            grouped = stream.tile([P, UNIT_NODES, PACK], BF16, name="ax_grouped", tag="ax_grouped", align_bytes=64)
+            ax_grouped[unit] = grouped
+            for k in range(UNIT_TILES):
+                nodes = slice(k * P, (k + 1) * P)
+                ax_bank = psum.tile([P, PACK, P], F32, name="ax_bank", tag="ax_bank")
+                for r in range(PACK):
+                    feats = slice(r * P, (r + 1) * P)
+                    for c in range(J_PASSES):
+                        nc.tensor.matmul_mx(
+                            out=ax_bank[:, r, :],
+                            lhsT=x_codes[g][:, c, feats].bitcast(FP8X4),
+                            lhsT_scale=x_scales[g][:, c, feats],
+                            rhs=adj_codes[unit][:, c, nodes].bitcast(FP8X4),
+                            rhs_scale=adj_scales[unit][:, c, nodes],
+                            start=(c == 0),
+                            stop=(c == J_PASSES - 1),
+                        )
+                nc.scalar.copy(out=grouped[:, nodes, :], in_=ax_bank[:].rearrange("p r m -> p m r"))
+
+        def quantise_ax(unit):
+            ax_codes[unit] = stream.tile([P, UNIT_NODES], U32, name="ax_codes", tag="ax_codes", align_bytes=64)
+            ax_scales[unit] = stream.tile([P, UNIT_NODES], U8, name="ax_scales", tag="ax_scales", align_bytes=64)
+            nc.vector.quantize_mx(
+                out=ax_codes[unit][:].bitcast(FP8X4),
+                scales=ax_scales[unit][:],
+                in_=ax_grouped[unit][:].rearrange("p m r -> p (m r)"),
+            )
+
+        def transform(unit):
+            results[unit] = stream.tile([P, UNIT_TILES, FEATS], F32, name="result", tag="result", bufs=5)
+            for k in range(UNIT_TILES):
+                nodes = slice(k * P, (k + 1) * P)
+                out_bank = psum.tile([P, FEATS], F32, name="out_bank", tag="out_bank")
+                nc.tensor.matmul_mx(
+                    out=out_bank[:],
+                    lhsT=ax_codes[unit][:, nodes].bitcast(FP8X4),
+                    lhsT_scale=ax_scales[unit][:, nodes],
+                    rhs=w_codes[:].bitcast(FP8X4),
+                    rhs_scale=w_plane[:],
+                    start=True,
+                    stop=True,
+                )
+                nc.vector.tensor_tensor(out=results[unit][:, k, :], in0=out_bank[:], in1=bias_all[:], op=ALU.add)
+
+        def finish(unit):
+            g = graph_of(unit)
+            first = first_tile_of(unit)
+            for k in range(UNIT_TILES):
+                a = first + k
+                tile_result = results[unit][:, k, :]
+                scale = reciprocals[g][:, a : a + 1]
+                if a % 4 == 3:
+                    nc.vector.tensor_scalar(
+                        out=tile_result, in0=tile_result, scalar1=0.0, scalar2=scale, op0=ALU.max, op1=ALU.mult
+                    )
+                else:
+                    nc.scalar.activation(out=tile_result, in_=tile_result, func=RELU, scale=scale)
+            by_tile = out[g].rearrange("(m a) n -> m a n", a=TILES)
+            nc.sync.dma_start(out=by_tile[:, first : first + UNIT_TILES, :], in_=results[unit][:])
+
+        def when_due(stage, unit):
+            if 0 <= unit < ALL_UNITS:
+                stage(unit)
+
+        def when_graph_due(stage, unit):
+            if 0 <= unit < ALL_UNITS and unit % UNITS_PER_GRAPH == 0:
+                stage(graph_of(unit))
+
+        for step in range(-X_LEAD, ALL_UNITS + LAG_FINISH):
+            when_due(finish, step - LAG_FINISH)
+            when_due(prepare_x, step + X_LEAD)
+            when_due(quantise_adj, step - LAG_QUANTISE_ADJ)
+            when_due(quantise_ax, step - LAG_QUANTISE_AX)
+            when_graph_due(collect_row_sums, step - LAG_RECIPROCAL)
+            when_due(transform, step - LAG_TRANSFORM)
+            when_due(aggregate, step - LAG_AGGREGATE)
+            when_graph_due(reciprocal_denominators, step - LAG_RECIPROCAL)
+            when_due(transpose_adj, step)
+            when_due(add_row_sums, step - LAG_QUANTISE_ADJ)

@@ -140,8 +140,8 @@ def tile_msamodel_pa_kernel(tc, x, adj, w_words, w_scales, b, out):
                     [P, J_PASSES, PACK, P, PACK], BF16, name="x_grouped", tag="x_grouped", bufs=2, align_bytes=64
                 )
             nc.vector.tensor_copy(
-                out=x_grouped[g][:, c],
-                in_=x_rows[(g, c)][:].rearrange("q t (p r) -> q r p t", r=PACK),
+                out=x_grouped[g][:, c].rearrange("q r p t -> q p t r"),
+                in_=x_rows[(g, c)][:].rearrange("q t (p r) -> q p t r", r=PACK),
             )
 
         def quantise_x(g):

@@ -27,13 +27,15 @@ ALL_UNITS = GRAPHS * UNITS_PER_GRAPH
 QUARTER = P // PACK
 QUARTERS = P // QUARTER
 
-LAG_QUANTISE_ADJ = 1
-LAG_AGGREGATE = 2
-LAG_QUANTISE_AX = 3
-LAG_TRANSFORM = 4
-LAG_RECIPROCAL = UNITS_PER_GRAPH + 1
-LAG_FINISH = LAG_RECIPROCAL + 1
+LAG_ROW_SUMS = 1
+LAG_QUANTISE_ADJ = 2
+LAG_AGGREGATE = 3
+LAG_QUANTISE_AX = 4
+LAG_TRANSFORM = 5
+LAG_RECIPROCAL = UNITS_PER_GRAPH + LAG_ROW_SUMS
+LAG_FINISH = 7
 X_LEAD = 1
+STAGE_BANKS = 6
 
 FLOPS = 2 * GRAPHS * NODES * NODES * FEATS + 2 * GRAPHS * NODES * FEATS * FEATS
 
@@ -45,7 +47,7 @@ def tile_msamodel_pa_kernel(tc, x, adj, w_words, w_scales, b, out):
         consts = ctx.enter_context(tc.tile_pool(name="consts", bufs=1))
         inputs = ctx.enter_context(tc.tile_pool(name="inputs", bufs=1))
         stream = ctx.enter_context(tc.tile_pool(name="stream", bufs=3))
-        psum = ctx.enter_context(tc.psum_pool(name="psum", bufs=2))
+        psum = ctx.enter_context(tc.psum_pool(name="psum", bufs=STAGE_BANKS))
 
         def graph_of(unit):
             return unit // UNITS_PER_GRAPH
@@ -115,7 +117,7 @@ def tile_msamodel_pa_kernel(tc, x, adj, w_words, w_scales, b, out):
                 op=ALU.add,
             )
 
-        bias_bank = psum.tile([P, FEATS], F32, name="bias_bank", tag="out_bank")
+        bias_bank = psum.tile([P, FEATS], F32, name="bias_bank", tag="bank")
         nc.tensor.matmul(out=bias_bank[:], lhsT=ones[:], rhs=bias_row[:], start=True, stop=True)
         bias_all = consts.tile([P, FEATS], F32)
         nc.scalar.copy(out=bias_all[:], in_=bias_bank[:])
@@ -164,11 +166,11 @@ def tile_msamodel_pa_kernel(tc, x, adj, w_words, w_scales, b, out):
         def transpose_adj(unit):
             words = adj_rows[unit][:].bitcast(F32)
             grouped = stream.tile(
-                [P, J_PASSES, UNIT_NODES, PACK], BF16, name="adj_grouped", tag="adj_grouped", align_bytes=64
+                [P, J_PASSES, UNIT_NODES, PACK], BF16, name="adj_grouped", tag="adj_grouped", bufs=4, align_bytes=64
             )
             adj_grouped[unit] = grouped
             for c in range(J_PASSES):
-                flipped = psum.tile([P, 2, UNIT_NODES], F32, name="flipped", tag="flipped")
+                flipped = psum.tile([P, 2, UNIT_NODES], F32, name="flipped", tag="bank")
                 for u in range(2):
                     block = 2 * c + u
                     for k in range(UNIT_TILES):
@@ -234,7 +236,7 @@ def tile_msamodel_pa_kernel(tc, x, adj, w_words, w_scales, b, out):
             ax_grouped[unit] = grouped
             for k in range(UNIT_TILES):
                 nodes = slice(k * P, (k + 1) * P)
-                ax_bank = psum.tile([P, PACK, P], F32, name="ax_bank", tag="ax_bank")
+                ax_bank = psum.tile([P, PACK, P], F32, name="ax_bank", tag="bank")
                 for r in range(PACK):
                     feats = slice(r * P, (r + 1) * P)
                     for c in range(J_PASSES):
@@ -259,10 +261,10 @@ def tile_msamodel_pa_kernel(tc, x, adj, w_words, w_scales, b, out):
             )
 
         def transform(unit):
-            results[unit] = stream.tile([P, UNIT_TILES, FEATS], F32, name="result", tag="result", bufs=5)
+            results[unit] = stream.tile([P, UNIT_TILES, FEATS], F32, name="result", tag="result", bufs=6)
             for k in range(UNIT_TILES):
                 nodes = slice(k * P, (k + 1) * P)
-                out_bank = psum.tile([P, FEATS], F32, name="out_bank", tag="out_bank")
+                out_bank = psum.tile([P, FEATS], F32, name="out_bank", tag="bank")
                 nc.tensor.matmul_mx(
                     out=out_bank[:],
                     lhsT=ax_codes[unit][:, nodes].bitcast(FP8X4),
@@ -308,4 +310,4 @@ def tile_msamodel_pa_kernel(tc, x, adj, w_words, w_scales, b, out):
             when_due(aggregate, step - LAG_AGGREGATE)
             when_graph_due(reciprocal_denominators, step - LAG_RECIPROCAL)
             when_due(transpose_adj, step)
-            when_due(add_row_sums, step - LAG_QUANTISE_ADJ)
+            when_due(add_row_sums, step - LAG_ROW_SUMS)

@@ -33,8 +33,9 @@ LAG_AGGREGATE = 3
 LAG_QUANTISE_AX = 4
 LAG_TRANSFORM = 5
 LAG_RECIPROCAL = UNITS_PER_GRAPH + LAG_ROW_SUMS
-LAG_FINISH = 7
-X_LEAD = 1
+LAG_FINISH = 6
+X_READY = LAG_AGGREGATE - 1
+ADJ_AHEAD_OF_X = 2
 STAGE_BANKS = 6
 
 FLOPS = 2 * GRAPHS * NODES * NODES * FEATS + 2 * GRAPHS * NODES * FEATS * FEATS
@@ -97,17 +98,13 @@ def tile_msamodel_pa_kernel(tc, x, adj, w_words, w_scales, b, out):
                 in_=w_words[0].rearrange("p n t -> p (n t)").bitcast(I32),
             )
 
-        load_x(0)
         nc.sync.dma_start(out=bias_row[0:1, :], in_=b.unsqueeze(0))
-        for unit in range(UNITS_PER_GRAPH):
+        for unit in range(ALL_UNITS):
             load_adj(unit)
-        load_x(1)
-        load_weight()
-        for g in range(1, GRAPHS):
-            for unit in range(g * UNITS_PER_GRAPH, (g + 1) * UNITS_PER_GRAPH):
-                load_adj(unit)
-            if g + 1 < GRAPHS:
-                load_x(g + 1)
+            if unit % UNITS_PER_GRAPH == ADJ_AHEAD_OF_X - 1:
+                load_x(graph_of(unit))
+            if unit == ADJ_AHEAD_OF_X:
+                load_weight()
 
         for s in range(QUARTERS):
             nc.vector.tensor_reduce(
@@ -155,10 +152,10 @@ def tile_msamodel_pa_kernel(tc, x, adj, w_words, w_scales, b, out):
                 in_=x_grouped[g][:].rearrange("q c r p t -> q (c r p t)"),
             )
 
-        def prepare_x(turn):
-            g = turn // UNITS_PER_GRAPH
-            part = turn % UNITS_PER_GRAPH
-            if part < J_PASSES:
+        def prepare_x(unit):
+            g = graph_of(unit)
+            part = unit % UNITS_PER_GRAPH + J_PASSES - X_READY
+            if 0 <= part < J_PASSES:
                 regroup_x(g, part)
             elif part == J_PASSES:
                 quantise_x(g)
@@ -300,14 +297,18 @@ def tile_msamodel_pa_kernel(tc, x, adj, w_words, w_scales, b, out):
             if 0 <= unit < ALL_UNITS and unit % UNITS_PER_GRAPH == 0:
                 stage(graph_of(unit))
 
-        for step in range(-X_LEAD, ALL_UNITS + LAG_FINISH):
+        for c in range(J_PASSES):
+            regroup_x(0, c)
+        quantise_x(0)
+        for step in range(ALL_UNITS + LAG_FINISH):
             when_due(finish, step - LAG_FINISH)
-            when_due(prepare_x, step + X_LEAD)
             when_due(quantise_adj, step - LAG_QUANTISE_ADJ)
             when_due(quantise_ax, step - LAG_QUANTISE_AX)
             when_graph_due(collect_row_sums, step - LAG_RECIPROCAL)
             when_due(transform, step - LAG_TRANSFORM)
             when_due(aggregate, step - LAG_AGGREGATE)
+            if step >= UNITS_PER_GRAPH:
+                when_due(prepare_x, step)
             when_graph_due(reciprocal_denominators, step - LAG_RECIPROCAL)
             when_due(transpose_adj, step)
             when_due(add_row_sums, step - LAG_ROW_SUMS)

@@ -34,8 +34,11 @@ LAG_QUANTISE_AX = 4
 LAG_TRANSFORM = 5
 LAG_RECIPROCAL = UNITS_PER_GRAPH + LAG_ROW_SUMS
 LAG_FINISH = 6
-X_READY = LAG_AGGREGATE - 1
+XQ = 4
+XL = 2
+XQL = 2
 ADJ_AHEAD_OF_X = 2
+AAX = 1
 STAGE_BANKS = 6
 
 FLOPS = 2 * GRAPHS * NODES * NODES * FEATS + 2 * GRAPHS * NODES * FEATS * FEATS
@@ -100,8 +103,10 @@ def tile_msamodel_pa_kernel(tc, x, adj, w_words, w_scales, b, out):
 
         nc.sync.dma_start(out=bias_row[0:1, :], in_=b.unsqueeze(0))
         for unit in range(ALL_UNITS):
+            if unit >= UNITS_PER_GRAPH and unit % UNITS_PER_GRAPH == AAX:
+                load_x(graph_of(unit))
             load_adj(unit)
-            if unit % UNITS_PER_GRAPH == ADJ_AHEAD_OF_X - 1:
+            if unit == ADJ_AHEAD_OF_X - 1:
                 load_x(graph_of(unit))
             if unit == ADJ_AHEAD_OF_X:
                 load_weight()
@@ -133,6 +138,23 @@ def tile_msamodel_pa_kernel(tc, x, adj, w_words, w_scales, b, out):
         ax_scales = {}
         results = {}
 
+        def regroup_x_slowly(g, c, quarter):
+            if c == 0 and quarter == 0:
+                x_grouped[g] = stream.tile(
+                    [P, J_PASSES, PACK, P, PACK], BF16, name="x_grouped", tag="x_grouped", bufs=2, align_bytes=64
+                )
+            part = slice(quarter * P // XQ, (quarter + 1) * P // XQ)
+            nc.gpsimd.tensor_scalar(
+                out=x_grouped[g][:, c, :, part, :].rearrange("q r p t -> q p t r"),
+                in0=x_rows[(g, c)][:, :, quarter * FEATS // XQ : (quarter + 1) * FEATS // XQ].rearrange(
+                    "q t (p r) -> q p t r", r=PACK
+                ),
+                scalar1=1.0,
+                scalar2=0.0,
+                op0=ALU.mult,
+                op1=ALU.add,
+            )
+
         def regroup_x(g, c):
             if c == 0:
                 x_grouped[g] = stream.tile(
@@ -154,11 +176,10 @@ def tile_msamodel_pa_kernel(tc, x, adj, w_words, w_scales, b, out):
 
         def prepare_x(unit):
             g = graph_of(unit)
-            part = unit % UNITS_PER_GRAPH + J_PASSES - X_READY
-            if 0 <= part < J_PASSES:
-                regroup_x(g, part)
-            elif part == J_PASSES:
-                quantise_x(g)
+            part = unit % UNITS_PER_GRAPH
+            n = 2 * XQ // 4
+            for i in range(part * n, (part + 1) * n):
+                regroup_x_slowly(g, i // XQ, i % XQ)
 
         def transpose_adj(unit):
             words = adj_rows[unit][:].bitcast(F32)
@@ -307,8 +328,11 @@ def tile_msamodel_pa_kernel(tc, x, adj, w_words, w_scales, b, out):
             when_graph_due(collect_row_sums, step - LAG_RECIPROCAL)
             when_due(transform, step - LAG_TRANSFORM)
             when_due(aggregate, step - LAG_AGGREGATE)
-            if step >= UNITS_PER_GRAPH:
-                when_due(prepare_x, step)
+            if step + XL >= UNITS_PER_GRAPH:
+                when_due(prepare_x, step + XL)
+            u = step - XQL
+            if UNITS_PER_GRAPH <= u < ALL_UNITS and u % UNITS_PER_GRAPH == 0:
+                quantise_x(graph_of(u))
             when_graph_due(reciprocal_denominators, step - LAG_RECIPROCAL)
             when_due(transpose_adj, step)
             when_due(add_row_sums, step - LAG_ROW_SUMS)

@@ -35,10 +35,11 @@ LAG_TRANSFORM = 5
 LAG_RECIPROCAL = UNITS_PER_GRAPH + LAG_ROW_SUMS
 LAG_FINISH = 6
 XQ = 4
+FINE_UNITS = 2
 XL = 2
 XQL = 2
 ADJ_AHEAD_OF_X = 2
-AAX = 1
+AAX = 0
 STAGE_BANKS = 6
 
 FLOPS = 2 * GRAPHS * NODES * NODES * FEATS + 2 * GRAPHS * NODES * FEATS * FEATS
@@ -108,7 +109,7 @@ def tile_msamodel_pa_kernel(tc, x, adj, w_words, w_scales, b, out):
             load_adj(unit)
             if unit == ADJ_AHEAD_OF_X - 1:
                 load_x(graph_of(unit))
-            if unit == ADJ_AHEAD_OF_X:
+            if unit == 4:
                 load_weight()
 
         for s in range(QUARTERS):
@@ -272,11 +273,15 @@ def tile_msamodel_pa_kernel(tc, x, adj, w_words, w_scales, b, out):
         def quantise_ax(unit):
             ax_codes[unit] = stream.tile([P, UNIT_NODES], U32, name="ax_codes", tag="ax_codes", align_bytes=64)
             ax_scales[unit] = stream.tile([P, UNIT_NODES], U8, name="ax_scales", tag="ax_scales", align_bytes=64)
-            nc.vector.quantize_mx(
-                out=ax_codes[unit][:].bitcast(FP8X4),
-                scales=ax_scales[unit][:],
-                in_=ax_grouped[unit][:].rearrange("p m r -> p (m r)"),
-            )
+            parts = UNIT_TILES if unit >= ALL_UNITS - FINE_UNITS else 1
+            width = UNIT_NODES // parts
+            for k in range(parts):
+                nodes = slice(k * width, (k + 1) * width)
+                nc.vector.quantize_mx(
+                    out=ax_codes[unit][:, nodes].bitcast(FP8X4),
+                    scales=ax_scales[unit][:, nodes],
+                    in_=ax_grouped[unit][:, nodes, :].rearrange("p m r -> p (m r)"),
+                )
 
         def transform(unit):
             results[unit] = stream.tile([P, UNIT_TILES, FEATS], F32, name="result", tag="result", bufs=6)
@@ -297,6 +302,7 @@ def tile_msamodel_pa_kernel(tc, x, adj, w_words, w_scales, b, out):
         def finish(unit):
             g = graph_of(unit)
             first = first_tile_of(unit)
+            by_tile = out[g].rearrange("(m a) n -> m a n", a=TILES)
             for k in range(UNIT_TILES):
                 a = first + k
                 tile_result = results[unit][:, k, :]
@@ -307,8 +313,10 @@ def tile_msamodel_pa_kernel(tc, x, adj, w_words, w_scales, b, out):
                     )
                 else:
                     nc.scalar.activation(out=tile_result, in_=tile_result, func=RELU, scale=scale)
-            by_tile = out[g].rearrange("(m a) n -> m a n", a=TILES)
-            nc.sync.dma_start(out=by_tile[:, first : first + UNIT_TILES, :], in_=results[unit][:])
+                if unit >= ALL_UNITS - FINE_UNITS:
+                    nc.sync.dma_start(out=by_tile[:, a : a + 1, :], in_=results[unit][:, k : k + 1, :])
+            if unit < ALL_UNITS - FINE_UNITS:
+                nc.sync.dma_start(out=by_tile[:, first : first + UNIT_TILES, :], in_=results[unit][:])
 
         def when_due(stage, unit):
             if 0 <= unit < ALL_UNITS:

@@ -40,7 +40,7 @@ XL = 2
 XQL = 2
 ADJ_AHEAD_OF_X = 2
 AAX = 0
-STAGE_BANKS = 6
+STAGE_BANKS = 7
 
 FLOPS = 2 * GRAPHS * NODES * NODES * FEATS + 2 * GRAPHS * NODES * FEATS * FEATS
 
@@ -132,6 +132,7 @@ def tile_msamodel_pa_kernel(tc, x, adj, w_words, w_scales, b, out):
         adj_codes = {}
         adj_scales = {}
         row_sums = {}
+        denominators = {}
         partial_sums = {}
         reciprocals = {}
         ax_grouped = {}
@@ -216,38 +217,38 @@ def tile_msamodel_pa_kernel(tc, x, adj, w_words, w_scales, b, out):
         def add_row_sums(unit):
             g = graph_of(unit)
             if unit % UNITS_PER_GRAPH == 0:
-                row_sums[g] = psum.tile([P, QUARTERS, TILES], F32, name="row_sums", tag="row_sums", bufs=1)
+                row_sums[g] = psum.tile([P, TILES * QUARTERS + 32], F32, name="row_sums", tag="row_sums", bufs=1)
             for k in range(UNIT_TILES):
                 a = first_tile_of(unit) + k
                 for s in range(QUARTERS):
                     first = k * P + s * QUARTER
                     for c in range(J_PASSES):
                         nc.tensor.matmul(
-                            out=row_sums[g][:, s, a : a + 1],
+                            out=row_sums[g][:, a * QUARTERS + s : a * QUARTERS + s + 32],
                             lhsT=adj_grouped[unit][:, c, first : first + QUARTER, :].rearrange("q w t -> q (w t)"),
-                            rhs=ones[:, 0:1],
+                            rhs=ones[:, 0:32],
                             start=(c == 0),
                             stop=(c == J_PASSES - 1),
                         )
 
         def collect_row_sums(g):
             partial_sums[g] = stream.tile([P, QUARTERS, TILES], F32, name="partial_sums", tag="partial_sums")
-            nc.vector.tensor_copy(out=partial_sums[g][:], in_=row_sums[g][:])
+            nc.vector.tensor_scalar_add(out=partial_sums[g][:], in0=row_sums[g][:, : TILES * QUARTERS].rearrange("p (a s) -> p s a", s=QUARTERS), scalar1=1.0 / PACK)
 
-        def reciprocal_denominators(g):
-            totals = psum.tile([P, TILES], F32, name="totals", tag="totals", bufs=1)
+        def add_partial_sums(g):
+            denominators[g] = psum.tile([P, TILES], F32, name="denominators", tag="bank")
             for s in range(QUARTERS):
                 nc.tensor.matmul(
-                    out=totals[:],
+                    out=denominators[g][:],
                     lhsT=selectors[:, s, :],
                     rhs=partial_sums[g][:, s, :],
                     start=(s == 0),
                     stop=(s == QUARTERS - 1),
                 )
-            denominators = stream.tile([P, TILES], F32, name="denominators", tag="denominators")
-            nc.vector.tensor_scalar_add(out=denominators[:], in0=totals[:], scalar1=1.0)
+
+        def take_reciprocals(g):
             reciprocals[g] = stream.tile([P, TILES], F32, name="reciprocals", tag="reciprocals")
-            nc.vector.reciprocal(out=reciprocals[g][:], in_=denominators[:])
+            nc.vector.reciprocal(out=reciprocals[g][:], in_=denominators[g][:])
 
         def aggregate(unit):
             g = graph_of(unit)
@@ -330,6 +331,7 @@ def tile_msamodel_pa_kernel(tc, x, adj, w_words, w_scales, b, out):
             regroup_x(0, c)
         quantise_x(0)
         for step in range(ALL_UNITS + LAG_FINISH):
+            when_graph_due(take_reciprocals, step - LAG_RECIPROCAL - 1)
             when_due(finish, step - LAG_FINISH)
             when_due(quantise_adj, step - LAG_QUANTISE_ADJ)
             when_due(quantise_ax, step - LAG_QUANTISE_AX)
@@ -341,6 +343,6 @@ def tile_msamodel_pa_kernel(tc, x, adj, w_words, w_scales, b, out):
             u = step - XQL
             if UNITS_PER_GRAPH <= u < ALL_UNITS and u % UNITS_PER_GRAPH == 0:
                 quantise_x(graph_of(u))
-            when_graph_due(reciprocal_denominators, step - LAG_RECIPROCAL)
+            when_graph_due(add_partial_sums, step - LAG_RECIPROCAL)
             when_due(transpose_adj, step)
             when_due(add_row_sums, step - LAG_ROW_SUMS)

from contextlib import ExitStack

import concourse.mybir as mybir
from concourse.masks import make_identity

BF16 = mybir.dt.bfloat16
F32 = mybir.dt.float32
I32 = mybir.dt.int32
U32 = mybir.dt.uint32
U8 = mybir.dt.uint8
FP8X4 = mybir.dt.float8_e4m3fn_x4
ALU = mybir.AluOpType
RELU = mybir.ActivationFunctionType.Relu

P = 128
PACK = 4
K_PASS = P * PACK
GRAPHS = 4
NODES = 1024
FEATS = 512
J_PASSES = NODES // K_PASS
TILES = NODES // P
UNIT_TILES = 2
UNIT_NODES = UNIT_TILES * P
UNITS_PER_GRAPH = TILES // UNIT_TILES
ALL_UNITS = GRAPHS * UNITS_PER_GRAPH
QUARTER = P // PACK
QUARTERS = P // QUARTER

LAG_ROW_SUMS = 1
LAG_QUANTISE_ADJ = 2
LAG_AGGREGATE = 3
LAG_QUANTISE_AX = 4
LAG_TRANSFORM = 5
LAG_RECIPROCAL = UNITS_PER_GRAPH + LAG_ROW_SUMS
LAG_FINISH = 6
XQ = 4
FINE_UNITS = 2
XL = 2
XQL = 2
ADJ_AHEAD_OF_X = 2
AAX = 0
STAGE_BANKS = 7

FLOPS = 2 * GRAPHS * NODES * NODES * FEATS + 2 * GRAPHS * NODES * FEATS * FEATS


def tile_msamodel_pa_kernel(tc, x, adj, w_words, w_scales, b, out):
    nc = tc.nc
    with ExitStack() as ctx:
        ctx.enter_context(tc.manual_schedule())
        consts = ctx.enter_context(tc.tile_pool(name="consts", bufs=1))
        inputs = ctx.enter_context(tc.tile_pool(name="inputs", bufs=1))
        stream = ctx.enter_context(tc.tile_pool(name="stream", bufs=3))
        psum = ctx.enter_context(tc.psum_pool(name="psum", bufs=STAGE_BANKS))

        def graph_of(unit):
            return unit // UNITS_PER_GRAPH

        def first_tile_of(unit):
            return (unit % UNITS_PER_GRAPH) * UNIT_TILES

        w_plane = consts.tile([P, FEATS], U8, align_bytes=64)
        nc.vector.memset(w_plane[:].bitcast(I32), 0)
        w_codes = consts.tile([P, FEATS * PACK], U8, align_bytes=64)
        selectors = consts.tile([P, QUARTERS, P], F32)
        nc.vector.memset(selectors[:], 0.0)
        bias_row = consts.tile([P, FEATS], BF16)
        nc.gpsimd.memset(bias_row[:], 0.0)
        ones = consts.tile([P, P], BF16)
        nc.gpsimd.memset(ones[:], 1.0)
        identity = consts.tile([P, P], F32)
        make_identity(nc, identity[:])

        x_rows = {}
        adj_rows = {}

        def load_x(g):
            for c in range(J_PASSES):
                rows = inputs.tile([P, PACK, FEATS], BF16, name="x_rows_%d_%d" % (g, c))
                x_rows[(g, c)] = rows
                nc.sync.dma_start(
                    out=rows[:].rearrange("q (u e) d -> q u (e d)", e=2),
                    in_=x[g, c * K_PASS : (c + 1) * K_PASS, :].rearrange("(u q e) d -> q u (e d)", q=P, e=2),
                )

        def load_adj(unit):
            first = first_tile_of(unit)
            rows = inputs.tile([P, UNIT_TILES, NODES], BF16, name="adj_rows_%d" % unit)
            adj_rows[unit] = rows
            by_tile = adj[graph_of(unit)].rearrange("(m a) j -> m a j", a=TILES)
            nc.sync.dma_start(out=rows[:], in_=by_tile[:, first : first + UNIT_TILES, :])

        def load_weight():
            for quadrant in range(PACK):
                nc.sync.dma_start(
                    out=w_plane[32 * quadrant : 32 * quadrant + PACK, :].bitcast(I32),
                    in_=w_scales[0, PACK * quadrant : PACK * (quadrant + 1), :].bitcast(I32),
                )
            nc.sync.dma_start(
                out=w_codes[:].bitcast(I32),
                in_=w_words[0].rearrange("p n t -> p (n t)").bitcast(I32),
            )

        nc.sync.dma_start(out=bias_row[0:1, :], in_=b.unsqueeze(0))
        for unit in range(ALL_UNITS):
            if unit >= UNITS_PER_GRAPH and unit % UNITS_PER_GRAPH == AAX:
                load_x(graph_of(unit))
            load_adj(unit)
            if unit == ADJ_AHEAD_OF_X - 1:
                load_x(graph_of(unit))
            if unit == 4:
                load_weight()

        for s in range(QUARTERS):
            nc.vector.tensor_reduce(
                out=selectors[:, s, s * QUARTER : (s + 1) * QUARTER],
                in_=identity[:].rearrange("k (r t) -> k r t", t=PACK),
                axis=mybir.AxisListType.X,
                op=ALU.add,
            )

        bias_bank = psum.tile([P, FEATS], F32, name="bias_bank", tag="bank")
        nc.tensor.matmul(out=bias_bank[:], lhsT=ones[:], rhs=bias_row[:], start=True, stop=True)
        bias_all = consts.tile([P, FEATS], F32)
        nc.scalar.copy(out=bias_all[:], in_=bias_bank[:])

        x_grouped = {}
        x_codes = {}
        x_scales = {}
        adj_grouped = {}
        adj_codes = {}
        adj_scales = {}
        row_sums = {}
        denominators = {}
        partial_sums = {}
        reciprocals = {}
        ax_grouped = {}
        ax_codes = {}
        ax_scales = {}
        results = {}

        def regroup_x_slowly(g, c, quarter):
            if c == 0 and quarter == 0:
                x_grouped[g] = stream.tile(
                    [P, J_PASSES, PACK, P, PACK], BF16, name="x_grouped", tag="x_grouped", bufs=2, align_bytes=64
                )
            part = slice(quarter * P // XQ, (quarter + 1) * P // XQ)
            nc.gpsimd.tensor_scalar(
                out=x_grouped[g][:, c, :, part, :].rearrange("q r p t -> q p t r"),
                in0=x_rows[(g, c)][:, :, quarter * FEATS // XQ : (quarter + 1) * FEATS // XQ].rearrange(
                    "q t (p r) -> q p t r", r=PACK
                ),
                scalar1=1.0,
                scalar2=0.0,
                op0=ALU.mult,
                op1=ALU.add,
            )

        def regroup_x(g, c):
            if c == 0:
                x_grouped[g] = stream.tile(
                    [P, J_PASSES, PACK, P, PACK], BF16, name="x_grouped", tag="x_grouped", bufs=2, align_bytes=64
                )
            nc.vector.tensor_copy(
                out=x_grouped[g][:, c].rearrange("q r p t -> q p t r"),
                in_=x_rows[(g, c)][:].rearrange("q t (p r) -> q p t r", r=PACK),
            )

        def quantise_x(g):
            x_codes[g] = stream.tile([P, J_PASSES, FEATS], U32, name="x_codes", tag="x_codes", bufs=2, align_bytes=64)
            x_scales[g] = stream.tile([P, J_PASSES, FEATS], U8, name="x_scales", tag="x_scales", bufs=2, align_bytes=64)
            nc.vector.quantize_mx(
                out=x_codes[g][:].rearrange("q c f -> q (c f)").bitcast(FP8X4),
                scales=x_scales[g][:].rearrange("q c f -> q (c f)"),
                in_=x_grouped[g][:].rearrange("q c r p t -> q (c r p t)"),
            )

        def prepare_x(unit):
            g = graph_of(unit)
            part = unit % UNITS_PER_GRAPH
            n = 2 * XQ // 4
            for i in range(part * n, (part + 1) * n):
                regroup_x_slowly(g, i // XQ, i % XQ)

        def transpose_adj(unit):
            words = adj_rows[unit][:].bitcast(F32)
            grouped = stream.tile(
                [P, J_PASSES, UNIT_NODES, PACK], BF16, name="adj_grouped", tag="adj_grouped", bufs=4, align_bytes=64
            )
            adj_grouped[unit] = grouped
            for c in range(J_PASSES):
                flipped = psum.tile([P, 2, UNIT_NODES], F32, name="flipped", tag="bank")
                for u in range(2):
                    block = 2 * c + u
                    for k in range(UNIT_TILES):
                        nc.tensor.transpose(
                            flipped[:, u, k * P : (k + 1) * P],
                            words[:, k, block * P : (block + 1) * P],
                            identity[:],
                        )
                nc.scalar.copy(out=grouped[:, c].bitcast(F32), in_=flipped[:].rearrange("q u w -> q w u"))

        def quantise_adj(unit):
            adj_codes[unit] = stream.tile(
                [P, J_PASSES, UNIT_NODES], U32, name="adj_codes", tag="adj_codes", bufs=4, align_bytes=64
            )
            adj_scales[unit] = stream.tile(
                [P, J_PASSES, UNIT_NODES], U8, name="adj_scales", tag="adj_scales", bufs=4, align_bytes=64
            )
            nc.vector.quantize_mx(
                out=adj_codes[unit][:].rearrange("q c w -> q (c w)").bitcast(FP8X4),
                scales=adj_scales[unit][:].rearrange("q c w -> q (c w)"),
                in_=adj_grouped[unit][:].rearrange("q c w t -> q (c w t)"),
            )

        def add_row_sums(unit):
            g = graph_of(unit)
            if unit % UNITS_PER_GRAPH == 0:
                row_sums[g] = psum.tile([P, TILES * QUARTERS + 32], F32, name="row_sums", tag="row_sums", bufs=1)
            for k in range(UNIT_TILES):
                a = first_tile_of(unit) + k
                for s in range(QUARTERS):
                    first = k * P + s * QUARTER
                    for c in range(J_PASSES):
                        nc.tensor.matmul(
                            out=row_sums[g][:, a * QUARTERS + s : a * QUARTERS + s + 32],
                            lhsT=adj_grouped[unit][:, c, first : first + QUARTER, :].rearrange("q w t -> q (w t)"),
                            rhs=ones[:, 0:32],
                            start=(c == 0),
                            stop=(c == J_PASSES - 1),
                        )

        def collect_row_sums(g):
            partial_sums[g] = stream.tile([P, QUARTERS, TILES], F32, name="partial_sums", tag="partial_sums")
            nc.vector.tensor_scalar_add(out=partial_sums[g][:], in0=row_sums[g][:, : TILES * QUARTERS].rearrange("p (a s) -> p s a", s=QUARTERS), scalar1=1.0 / PACK)

        def add_partial_sums(g):
            denominators[g] = psum.tile([P, TILES], F32, name="denominators", tag="bank")
            for s in range(QUARTERS):
                nc.tensor.matmul(
                    out=denominators[g][:],
                    lhsT=selectors[:, s, :],
                    rhs=partial_sums[g][:, s, :],
                    start=(s == 0),
                    stop=(s == QUARTERS - 1),
                )

        def take_reciprocals(g):
            reciprocals[g] = stream.tile([P, TILES], F32, name="reciprocals", tag="reciprocals")
            nc.vector.reciprocal(out=reciprocals[g][:], in_=denominators[g][:])

        def aggregate(unit):
            g = graph_of(unit)
            grouped = stream.tile([P, UNIT_NODES, PACK], BF16, name="ax_grouped", tag="ax_grouped", align_bytes=64)
            ax_grouped[unit] = grouped
            for k in range(UNIT_TILES):
                nodes = slice(k * P, (k + 1) * P)
                ax_bank = psum.tile([P, PACK, P], F32, name="ax_bank", tag="bank")
                for r in range(PACK):
                    feats = slice(r * P, (r + 1) * P)
                    for c in range(J_PASSES):
                        nc.tensor.matmul_mx(
                            out=ax_bank[:, r, :],
                            lhsT=x_codes[g][:, c, feats].bitcast(FP8X4),
                            lhsT_scale=x_scales[g][:, c, feats],
                            rhs=adj_codes[unit][:, c, nodes].bitcast(FP8X4),
                            rhs_scale=adj_scales[unit][:, c, nodes],
                            start=(c == 0),
                            stop=(c == J_PASSES - 1),
                        )
                nc.scalar.copy(out=grouped[:, nodes, :], in_=ax_bank[:].rearrange("p r m -> p m r"))

        def quantise_ax(unit):
            ax_codes[unit] = stream.tile([P, UNIT_NODES], U32, name="ax_codes", tag="ax_codes", align_bytes=64)
            ax_scales[unit] = stream.tile([P, UNIT_NODES], U8, name="ax_scales", tag="ax_scales", align_bytes=64)
            parts = UNIT_TILES if unit >= ALL_UNITS - FINE_UNITS else 1
            width = UNIT_NODES // parts
            for k in range(parts):
                nodes = slice(k * width, (k + 1) * width)
                nc.vector.quantize_mx(
                    out=ax_codes[unit][:, nodes].bitcast(FP8X4),
                    scales=ax_scales[unit][:, nodes],
                    in_=ax_grouped[unit][:, nodes, :].rearrange("p m r -> p (m r)"),
                )

        def transform(unit):
            results[unit] = stream.tile([P, UNIT_TILES, FEATS], F32, name="result", tag="result", bufs=6)
            for k in range(UNIT_TILES):
                nodes = slice(k * P, (k + 1) * P)
                out_bank = psum.tile([P, FEATS], F32, name="out_bank", tag="bank")
                nc.tensor.matmul_mx(
                    out=out_bank[:],
                    lhsT=ax_codes[unit][:, nodes].bitcast(FP8X4),
                    lhsT_scale=ax_scales[unit][:, nodes],
                    rhs=w_codes[:].bitcast(FP8X4),
                    rhs_scale=w_plane[:],
                    start=True,
                    stop=True,
                )
                nc.vector.tensor_tensor(out=results[unit][:, k, :], in0=out_bank[:], in1=bias_all[:], op=ALU.add)

        def finish(unit):
            g = graph_of(unit)
            first = first_tile_of(unit)
            by_tile = out[g].rearrange("(m a) n -> m a n", a=TILES)
            for k in range(UNIT_TILES):
                a = first + k
                tile_result = results[unit][:, k, :]
                scale = reciprocals[g][:, a : a + 1]
                if a % 4 == 3:
                    nc.vector.tensor_scalar(
                        out=tile_result, in0=tile_result, scalar1=0.0, scalar2=scale, op0=ALU.max, op1=ALU.mult
                    )
                else:
                    nc.scalar.activation(out=tile_result, in_=tile_result, func=RELU, scale=scale)
                if unit >= ALL_UNITS - FINE_UNITS:
                    nc.sync.dma_start(out=by_tile[:, a : a + 1, :], in_=results[unit][:, k : k + 1, :])
            if unit < ALL_UNITS - FINE_UNITS:
                nc.sync.dma_start(out=by_tile[:, first : first + UNIT_TILES, :], in_=results[unit][:])

        def when_due(stage, unit):
            if 0 <= unit < ALL_UNITS:
                stage(unit)

        def when_graph_due(stage, unit):
            if 0 <= unit < ALL_UNITS and unit % UNITS_PER_GRAPH == 0:
                stage(graph_of(unit))

        for c in range(J_PASSES):
            regroup_x(0, c)
        quantise_x(0)
        for step in range(ALL_UNITS + LAG_FINISH):
            when_graph_due(take_reciprocals, step - LAG_RECIPROCAL - 1)
            when_due(finish, step - LAG_FINISH)
            when_due(quantise_adj, step - LAG_QUANTISE_ADJ)
            when_due(quantise_ax, step - LAG_QUANTISE_AX)
            when_graph_due(collect_row_sums, step - LAG_RECIPROCAL)
            when_due(transform, step - LAG_TRANSFORM)
            when_due(aggregate, step - LAG_AGGREGATE)
            if step + XL >= UNITS_PER_GRAPH:
                when_due(prepare_x, step + XL)
            u = step - XQL
            if UNITS_PER_GRAPH <= u < ALL_UNITS and u % UNITS_PER_GRAPH == 0:
                quantise_x(graph_of(u))
            when_graph_due(add_partial_sums, step - LAG_RECIPROCAL)
            when_due(transpose_adj, step)
            when_due(add_row_sums, step - LAG_ROW_SUMS)
